import numpy as np
import ml_dtypes


def mxq(x, axis, fmt="e4m3"):
    dtype, down = {"e4m3": (ml_dtypes.float8_e4m3fn, 7), "e5m2": (ml_dtypes.float8_e5m2, 14)}[fmt]
    v = np.moveaxis(np.asarray(x, np.float32).astype(ml_dtypes.bfloat16).astype(np.float64), axis, -1)
    blocks = v.reshape(v.shape[:-1] + (-1, 32))
    amax = np.abs(blocks).max(-1, keepdims=True)
    byte = np.maximum(np.where(amax > 0, np.frexp(amax)[1] - 1 + 127, 0) - down, 1)
    scale = np.exp2(byte - 127.0)
    codes = (blocks / scale).astype(np.float32).astype(dtype).astype(np.float64)
    return np.moveaxis((codes * scale).reshape(v.shape), -1, axis)


WIDE = False


def mx_kscale(k):
    if not WIDE:
        return np.ones(k)
    levels = np.array([10, -10, 5, -5, 0])
    if k % 512:
        return np.exp2(np.random.permutation(np.resize(levels, k // 32))).repeat(32)
    a = np.empty((k // 512, 16))
    for p in range(k // 512):
        a[p, :8] = np.random.permutation(np.resize(levels, 8))
        for g in range(8):
            far = levels[np.abs(levels - a[p, g]) >= 10]
            a[p, g + 8] = far[np.random.randint(len(far))]
    return np.exp2(a.ravel()).repeat(32)


BF16 = ml_dtypes.bfloat16


def bf(x):
    return np.asarray(x, np.float32).astype(BF16)


def f64(x):
    return np.asarray(x).astype(np.float64)


B, S, D, H = 4, 1024, 512, 4
DH = D // H
ROPE_BASE = 10000.0


def rope_split(x, freqs_cis):
    b, s, h, dh = x.shape
    xr = x.reshape(b, s, h, dh // 2, 2)
    x_real, x_imag = xr[..., 0], xr[..., 1]
    fc = freqs_cis[:s][:, None, :, :]
    cos, sin = fc[..., 0], fc[..., 1]
    rot_real = x_real * cos - x_imag * sin
    rot_imag = x_real * sin + x_imag * cos
    return np.concatenate([rot_real, rot_imag], axis=-1)


def draw0():
    s = mx_kscale(D)
    inv_freq = 1.0 / ROPE_BASE ** (np.arange(0, DH, 2) / DH)
    ang = np.outer(np.arange(S), inv_freq)
    return {"hidden_states": bf(np.random.standard_normal((B, S, D)) * s),
            "freqs_cis": bf(np.stack([np.cos(ang), np.sin(ang)], axis=-1)),
            "Wq": bf(np.random.standard_normal((D, D)) / np.sqrt(D) / s),
            "bq": bf(np.random.standard_normal(D) * 0.3),
            "Wk": bf(np.random.standard_normal((D, D)) / np.sqrt(D) / s),
            "bk": bf(np.random.standard_normal(D) * 0.3)}


def core(hidden_states, freqs_cis, Wq, bq, Wk, bk):
    x = f64(hidden_states)
    b, s, _ = x.shape
    fc = f64(freqs_cis)
    xq = mxq(x, 2, "e4m3")
    q = ((xq @ mxq(f64(Wq), 1, "e4m3").T) + f64(bq)).reshape(b, s, H, DH)
    k = ((xq @ mxq(f64(Wk), 1, "e4m3").T) + f64(bk)).reshape(b, s, H, DH)
    return rope_split(q, fc), rope_split(k, fc)


def e4m3fn_bytes(y):
    return np.clip(np.asarray(y, np.float64), -448.0, 448.0).astype(np.float32).astype(ml_dtypes.float8_e4m3fn).view(np.uint8)


def e4m3fn_values(b):
    return np.asarray(b, np.uint8).view(ml_dtypes.float8_e4m3fn).astype(np.float64)


def setup_inputs():
    d = draw0()
    x0 = np.asarray(d['hidden_states']).astype(np.float64)
    s = (np.max(np.abs(x0), axis=(0, 1), keepdims=True) / 448.0).astype(np.float32)
    out = {}
    for k, v in d.items():
        if k == 'hidden_states':
            out['hidden_states_bytes'] = e4m3fn_bytes(x0 / s.astype(np.float64))
            out['hidden_states_scale'] = s
        else:
            out[k] = v
    return out


def reference(hidden_states_bytes, hidden_states_scale, freqs_cis, Wq, bq, Wk, bk):
    return core(e4m3fn_values(hidden_states_bytes) * hidden_states_scale.astype(np.float64), freqs_cis, Wq, bq, Wk, bk)

@@ -1,0 +1,270 @@
+from contextlib import ExitStack
+
+import concourse.mybir as mybir
+from concourse.masks import make_identity
+
+F32 = mybir.dt.float32
+BF16 = mybir.dt.bfloat16
+U8 = mybir.dt.uint8
+U32 = mybir.dt.uint32
+FP8 = mybir.dt.float8_e4m3fn
+FP8X4 = mybir.dt.float8_e4m3fn_x4
+ALU = mybir.AluOpType
+ACT = mybir.ActivationFunctionType
+
+B, S, D, H = 4, 1024, 512, 4
+FLOPS = 2 * B * S * D * 2 * D
+
+P = 128
+CHUNK = 512
+N_CHUNKS = B * S // CHUNK
+LAG = 3
+
+
+def tile_attention_pa_t_kernel(tc, x_bytes, x_scale, freqs, wq, bq, wk, bk, out_q, out_k):
+    nc = tc.nc
+    with ExitStack() as ctx:
+        const = ctx.enter_context(tc.tile_pool(name="const", bufs=1))
+        xin = ctx.enter_context(tc.tile_pool(name="xin", bufs=1))
+        xw = ctx.enter_context(tc.tile_pool(name="xw", bufs=2))
+        work = ctx.enter_context(tc.tile_pool(name="work", bufs=6))
+        outp = ctx.enter_context(tc.tile_pool(name="outp", bufs=3))
+        ps_mx = ctx.enter_context(tc.psum_pool(name="ps_mx", bufs=4))
+        ps_tp = ctx.enter_context(tc.psum_pool(name="ps_tp", bufs=4))
+
+        x_view = x_bytes.rearrange("b s k -> (b s) k").rearrange("(c p a) k -> c p (a k)", p=P, a=4)
+        o_views = [
+            o.rearrange("b s h d -> (b s) (h d)").rearrange("(c p a) f -> c p (a f)", p=P, a=4)
+            for o in (out_q, out_k)
+        ]
+
+        xraw = []
+        for c in range(N_CHUNKS):
+            xraw.append(xin.tile([P, 4 * D], U8, name="xraw%d" % c))
+        nc.sync.dma_start(out=xraw[0][:], in_=x_view[0])
+        fraw = const.tile([P, 2, 4, 2, 128], BF16, name="fraw")
+        f_view = freqs.rearrange("(i p a) j e -> i p a (j e)", p=P, a=4)
+        for hh in range(2):
+            nc.sync.dma_start(out=fraw[:, 0, :, hh, :], in_=f_view[0])
+        sc4 = const.tile([P, 4], F32, name="sc4")
+        nc.sync.dma_start(out=sc4[:], in_=x_scale.rearrange("o n (p t) -> p (o n t)", t=4))
+        wraw = const.tile([P, 2, 2, 2 * D], BF16, name="wraw")
+        nc.sync.dma_start(out=wraw[:, 0], in_=wq.rearrange("(g m e) k -> m g (e k)", m=P, e=2))
+        braw_q = const.tile([P, 2, 2], BF16, name="braw_q")
+        nc.sync.dma_start(out=braw_q[:], in_=bq.rearrange("(g m e) -> m g e", m=P, e=2))
+        braw_k = const.tile([P, 2, 2], BF16, name="braw_k")
+        nc.sync.dma_start(out=braw_k[:], in_=bk.rearrange("(g m e) -> m g e", m=P, e=2))
+        nc.sync.dma_start(out=wraw[:, 1], in_=wk.rearrange("(g m e) k -> m g (e k)", m=P, e=2))
+        for hh in range(2):
+            nc.sync.dma_start(out=fraw[:, 1, :, hh, :], in_=f_view[1])
+        for c in range(1, N_CHUNKS):
+            nc.sync.dma_start(out=xraw[c][:], in_=x_view[c])
+
+        ident = const.tile([P, P], F32, name="ident")
+        make_identity(nc, ident[:])
+        ident_bf = const.tile([P, P], BF16, name="ident_bf")
+        make_identity(nc, ident_bf[:])
+
+        bias = const.tile([P, 2, 2, 2], F32, name="bias")
+        for qk, braw in enumerate((braw_q, braw_k)):
+            nc.vector.tensor_copy(out=bias[:, qk], in_=braw[:])
+
+        sc_b = sc4[:].rearrange("p (o u e) -> p o u e", o=1, u=2).to_broadcast([P, 256, 2, 2])
+        xstate = {}
+
+        def x_cast(c, h):
+            if h == 0:
+                xstate[("bf", c)] = xw.tile([P, 4 * D], BF16, name="xbf")
+            cols = slice(h * 1024, (h + 1) * 1024)
+            nc.scalar.copy(out=xstate[("bf", c)][:, cols], in_=xraw[c][:, cols].bitcast(FP8))
+
+        def x_turn(c, h):
+            if h == 0:
+                xstate[("g", c)] = xw.tile([P, 4 * CHUNK], BF16, name="xg", align_bytes=64)
+            words = xstate[("bf", c)][:].bitcast(F32)
+            xt = ps_tp.tile([P, 2, 256], F32, name="xt", tag="tp")
+            for aa in range(2):
+                a = 2 * h + aa
+                for u in range(2):
+                    nc.tensor.transpose(
+                        xt[:, u, aa * P : (aa + 1) * P], words[:, a * 256 + u : (a + 1) * 256 : 2], ident[:]
+                    )
+            nc.vector.tensor_tensor(
+                out=xstate[("g", c)][:, h * 1024 : (h + 1) * 1024].rearrange("p (n u e) -> p n u e", u=2, e=2),
+                in0=xt[:].bitcast(BF16).rearrange("p u (n e) -> p n u e", e=2),
+                in1=sc_b,
+                op=ALU.mult,
+            )
+
+        def x_quant(c):
+            xc = xw.tile([P, CHUNK], U32, name="xc", align_bytes=64)
+            xs = xw.tile([P, CHUNK], U8, name="xs", align_bytes=64)
+            nc.vector.quantize_mx(out=xc[:].bitcast(FP8X4), scales=xs[:], in_=xstate[("g", c)][:])
+            xstate[("q", c)] = (xc, xs)
+
+        wg = const.tile([P, 2 * 2048], BF16, name="wg", align_bytes=64)
+        wc = const.tile([P, 2 * 512], U32, name="wc", align_bytes=64)
+        ws = const.tile([P, 2 * 512], U8, name="ws", align_bytes=64)
+
+        def w_prep(qk):
+            words = wraw[:, qk].rearrange("p g f -> p (g f)").bitcast(F32)
+            for g in range(2):
+                wt = ps_tp.tile([P, 2, 256], F32, name="wt", tag="tp")
+                for e in range(2):
+                    ti = 2 * g + e
+                    for u in range(2):
+                        nc.tensor.transpose(
+                            wt[:, u, e * P : (e + 1) * P], words[:, ti * 256 + u : (ti + 1) * 256 : 2], ident[:]
+                        )
+                lo = qk * 2048 + g * 1024
+                nc.scalar.copy(
+                    out=wg[:, lo : lo + 1024].bitcast(F32).rearrange("p (n u) -> p n u", u=2),
+                    in_=wt[:].rearrange("p u n -> p n u"),
+                )
+            nc.vector.quantize_mx(
+                out=wc[:, qk * 512 : (qk + 1) * 512].bitcast(FP8X4),
+                scales=ws[:, qk * 512 : (qk + 1) * 512],
+                in_=wg[:, qk * 2048 : (qk + 1) * 2048],
+            )
+
+        tabs = const.tile([P, 2, 3, CHUNK], F32, name="tabs")
+        fr = fraw[:].rearrange("p i a hh (j e) -> p i a (hh j) e", e=2)
+
+        def tables_turn(i):
+            for e in (0, 1):
+                tt = ps_tp.tile([P, CHUNK], BF16, name="tt", tag="tp")
+                for a in range(4):
+                    nc.tensor.transpose(tt[:, a * P : (a + 1) * P], fr[:, i, a, :, e], ident_bf[:])
+                if e == 0:
+                    nc.scalar.activation(out=tabs[:, i, 1, :], in_=tt[:], func=ACT.Copy, scale=1.0)
+                else:
+                    nc.scalar.activation(out=tabs[:, i, 2, :], in_=tt[:], func=ACT.Copy, scale=-1.0)
+                    nc.scalar.activation(out=tabs[:, i, 0, :], in_=tt[:], func=ACT.Copy, scale=1.0)
+
+        steps = [(c, qk, g) for c in range(N_CHUNKS) for qk in range(2) for g in range(2)]
+        n_steps = len(steps)
+        live = {}
+        otiles = {}
+
+        def v_takes(n):
+            return n % 4 >= 2
+
+        def front_mx(n):
+            c, qk, g = steps[n]
+            xc, xs = xstate[("q", c)]
+            base = qk * 512 + g * 256
+            accs = []
+            for e, nm in ((1, "xb"), (0, "xa")):
+                cols = slice(base + e * P, base + (e + 1) * P)
+                acc = ps_mx.tile([P, CHUNK], F32, name=nm, tag="mx")
+                nc.tensor.matmul_mx(
+                    out=acc[:],
+                    lhsT=wc[:, cols].bitcast(FP8X4),
+                    lhsT_scale=ws[:, cols],
+                    rhs=xc[:].bitcast(FP8X4),
+                    rhs_scale=xs[:],
+                    start=True,
+                    stop=True,
+                )
+                accs.append(acc)
+            live[("x", n)] = accs
+
+        def front_mul(n):
+            c, qk, g = steps[n]
+            i = c % 2
+            xb, xa = live[("x", n)]
+            def vpair(acc, e, slots, nm):
+                k = work.tile([P, 2, CHUNK], F32, name=nm)
+                nc.vector.scalar_tensor_tensor(
+                    out=k[:],
+                    in0=acc[:].rearrange("p (o n) -> p o n", o=1).to_broadcast([P, 2, CHUNK]),
+                    scalar=bias[:, qk, g, e : e + 1],
+                    in1=tabs[:, i, slots, :],
+                    op0=ALU.add,
+                    op1=ALU.mult,
+                )
+                return k
+
+            re = None
+            if v_takes(n):
+                vb = vpair(xb, 1, slice(1, 3), "vb")
+                ga = vpair(xa, 0, slice(0, 2), "ga")
+                if n < n_steps - 2:
+                    re = work.tile([P, CHUNK], F32, name="re")
+                    nc.gpsimd.tensor_tensor(out=re[:], in0=ga[:, 1, :], in1=vb[:, 1, :], op=ALU.add)
+            else:
+                a1 = work.tile([P, CHUNK], F32, name="a1")
+                nc.scalar.activation(out=a1[:], in_=xa[:], func=ACT.Identity, bias=bias[:, qk, g, 0:1], scale=1.0)
+                vb = vpair(xb, 1, slice(1, 3), "vb")
+                ga = work.tile([P, 2, CHUNK], F32, name="ga")
+                for slot in (1, 0):
+                    nc.gpsimd.tensor_tensor(out=ga[:, slot, :], in0=a1[:], in1=tabs[:, i, slot, :], op=ALU.mult)
+            live[("k", n)] = (
+                (ga[:, 1, :], vb[:, 1, :]) if re is None else (re[:],),
+                (ga[:, 0, :], vb[:, 0, :]),
+            )
+
+        def back(n):
+            c, qk, g = steps[n]
+            if g == 0:
+                otiles[(c, qk)] = outp.tile([P, 4, D], F32, name="o")
+            o = otiles[(c, qk)]
+            ov = o[:].rearrange("p a (g hh half j) -> p a g hh half j", g=2, hh=2, half=2)
+            last = n >= n_steps - 2
+            for half in range(2):
+                tp = ps_tp.tile([P, CHUNK], F32, name="bt", tag="tp")
+                for a in range(4):
+                    blk = slice(a * P, (a + 1) * P)
+                    terms = live[("k", n)][half]
+                    for ti, t in enumerate(terms):
+                        nc.tensor.matmul(
+                            out=tp[:, blk],
+                            lhsT=t[:, blk],
+                            rhs=ident[:],
+                            is_transpose=True,
+                            start=(ti == 0),
+                            stop=(ti == len(terms) - 1),
+                        )
+                dst = ov[:, :, g, :, half, :]
+                srcv = tp[:].rearrange("p (a hh j) -> p a hh j", a=4, hh=2)
+                if last and half == 1:
+                    nc.vector.tensor_copy(out=dst, in_=srcv)
+                else:
+                    nc.scalar.copy(out=dst, in_=srcv)
+            if last:
+                nc.sync.dma_start(
+                    out=o_views[qk][c].rearrange("p (a g f) -> p a g f", a=4, g=2)[:, :, g, :],
+                    in_=o[:].rearrange("p a (g f) -> p a g f", g=2)[:, :, g, :],
+                )
+            elif g == 1:
+                nc.sync.dma_start(out=o_views[qk][c], in_=o[:].rearrange("p a f -> p (a f)"))
+
+        x_cast(0, 0)
+        x_cast(0, 1)
+        tables_turn(0)
+        x_turn(0, 0)
+        x_turn(0, 1)
+        w_prep(0)
+        x_quant(0)
+        tables_turn(1)
+        w_prep(1)
+        x_cast(1, 0)
+        x_cast(1, 1)
+
+        for n in range(n_steps + LAG):
+            if n < n_steps:
+                front_mx(n)
+                front_mul(n)
+            if n >= LAG:
+                back(n - LAG)
+            c_next = n // 4 + 1
+            if c_next < N_CHUNKS:
+                if n % 4 == 0:
+                    x_turn(c_next, 0)
+                elif n % 4 == 1:
+                    x_turn(c_next, 1)
+                else:
+                    if n % 4 == 2:
+                        x_quant(c_next)
+                    if c_next + 1 < N_CHUNKS:
+                        x_cast(c_next + 1, n % 4 - 2)

@@ -251,20 +251,21 @@ def tile_attention_pa_t_kernel(tc, x_bytes, x_scale, freqs, wq, bq, wk, bk, out_
         x_cast(1, 0)
         x_cast(1, 1)
 
-        for n in range(n_steps + LAG):
-            if n < n_steps:
-                front_mx(n)
-                front_mul(n)
-            if n >= LAG:
-                back(n - LAG)
-            c_next = n // 4 + 1
-            if c_next < N_CHUNKS:
-                if n % 4 == 0:
-                    x_turn(c_next, 0)
-                elif n % 4 == 1:
-                    x_turn(c_next, 1)
-                else:
-                    if n % 4 == 2:
-                        x_quant(c_next)
-                    if c_next + 1 < N_CHUNKS:
-                        x_cast(c_next + 1, n % 4 - 2)
+        with tc.manual_schedule(engines={mybir.EngineType.PE}):
+            for n in range(n_steps + LAG):
+                if n < n_steps:
+                    front_mx(n)
+                    front_mul(n)
+                if n >= LAG:
+                    back(n - LAG)
+                c_next = n // 4 + 1
+                if c_next < N_CHUNKS:
+                    if n % 4 == 0:
+                        x_turn(c_next, 0)
+                    elif n % 4 == 1:
+                        x_turn(c_next, 1)
+                    else:
+                        if n % 4 == 2:
+                            x_quant(c_next)
+                        if c_next + 1 < N_CHUNKS:
+                            x_cast(c_next + 1, n % 4 - 2)

@@ -29,8 +29,8 @@ def tile_attention_pa_t_kernel(tc, x_bytes, x_scale, freqs, wq, bq, wk, bk, out_
         xw = ctx.enter_context(tc.tile_pool(name="xw", bufs=2))
         work = ctx.enter_context(tc.tile_pool(name="work", bufs=6))
         outp = ctx.enter_context(tc.tile_pool(name="outp", bufs=3))
-        ps_mx = ctx.enter_context(tc.psum_pool(name="ps_mx", bufs=4))
-        ps_tp = ctx.enter_context(tc.psum_pool(name="ps_tp", bufs=4))
+        ps_mx = ctx.enter_context(tc.psum_pool(name="ps_mx", bufs=5))
+        ps_tp = ctx.enter_context(tc.psum_pool(name="ps_tp", bufs=3))
 
         x_view = x_bytes.rearrange("b s k -> (b s) k").rearrange("(c p a) k -> c p (a k)", p=P, a=4)
         o_views = [
@@ -147,7 +147,7 @@ def tile_attention_pa_t_kernel(tc, x_bytes, x_scale, freqs, wq, bq, wk, bk, out_
         otiles = {}
 
         def v_takes(n):
-            return n % 4 >= 2
+            return n % 2 == 1 or n >= n_steps - 2
 
         def front_mx(n):
             c, qk, g = steps[n]
@@ -250,22 +250,24 @@ def tile_attention_pa_t_kernel(tc, x_bytes, x_scale, freqs, wq, bq, wk, bk, out_
         w_prep(1)
         x_cast(1, 0)
         x_cast(1, 1)
+        x_turn(1, 0)
 
+        n_halves = 2 * N_CHUNKS
         with tc.manual_schedule(engines={mybir.EngineType.PE}):
-            for n in range(n_steps + LAG):
-                if n < n_steps:
-                    front_mx(n)
-                    front_mul(n)
-                if n >= LAG:
-                    back(n - LAG)
-                c_next = n // 4 + 1
-                if c_next < N_CHUNKS:
-                    if n % 4 == 0:
-                        x_turn(c_next, 0)
-                    elif n % 4 == 1:
-                        x_turn(c_next, 1)
-                    else:
-                        if n % 4 == 2:
-                            x_quant(c_next)
-                        if c_next + 1 < N_CHUNKS:
-                            x_cast(c_next + 1, n % 4 - 2)
+            for k in range((n_steps + LAG + 1) // 2):
+                pair = (2 * k, 2 * k + 1)
+                for n in pair:
+                    if n < n_steps:
+                        front_mx(n)
+                if k % 2 == 1 and (k + 1) // 2 < N_CHUNKS:
+                    x_quant((k + 1) // 2)
+                for n in pair:
+                    if n < n_steps:
+                        front_mul(n)
+                for n in pair:
+                    if LAG <= n < n_steps + LAG:
+                        back(n - LAG)
+                if k + 3 < n_halves:
+                    x_turn((k + 3) // 2, (k + 3) % 2)
+                if k + 4 < n_halves:
+                    x_cast((k + 4) // 2, (k + 4) % 2)

@@ -189,9 +189,6 @@ def tile_attention_pa_t_kernel(tc, x_bytes, x_scale, freqs, wq, bq, wk, bk, out_
             if v_takes(n):
                 vb = vpair(xb, 1, slice(1, 3), "vb")
                 ga = vpair(xa, 0, slice(0, 2), "ga")
-                if n < n_steps - 2:
-                    re = work.tile([P, CHUNK], F32, name="re")
-                    nc.gpsimd.tensor_tensor(out=re[:], in0=ga[:, 1, :], in1=vb[:, 1, :], op=ALU.add)
             else:
                 a1 = work.tile([P, CHUNK], F32, name="a1")
                 nc.scalar.activation(out=a1[:], in_=xa[:], func=ACT.Identity, bias=bias[:, qk, g, 0:1], scale=1.0)

@@ -147,7 +147,7 @@ def tile_attention_pa_t_kernel(tc, x_bytes, x_scale, freqs, wq, bq, wk, bk, out_
         otiles = {}
 
         def v_takes(n):
-            return n % 2 == 1 or n >= n_steps - 2
+            return (n % 2 == 1 and n % 8 != 3) or n >= n_steps - 2
 
         def front_mx(n):
             c, qk, g = steps[n]

@@ -24,9 +24,10 @@ LAG = 3
 def tile_attention_pa_t_kernel(tc, x_bytes, x_scale, freqs, wq, bq, wk, bk, out_q, out_k):
     nc = tc.nc
     with ExitStack() as ctx:
+        ctx.enter_context(tc.manual_schedule())
         const = ctx.enter_context(tc.tile_pool(name="const", bufs=1))
         xin = ctx.enter_context(tc.tile_pool(name="xin", bufs=1))
-        xw = ctx.enter_context(tc.tile_pool(name="xw", bufs=2))
+        xw = ctx.enter_context(tc.tile_pool(name="xw", bufs=3))
         work = ctx.enter_context(tc.tile_pool(name="work", bufs=6))
         outp = ctx.enter_context(tc.tile_pool(name="outp", bufs=3))
         ps_mx = ctx.enter_context(tc.psum_pool(name="ps_mx", bufs=5))
@@ -42,22 +43,23 @@ def tile_attention_pa_t_kernel(tc, x_bytes, x_scale, freqs, wq, bq, wk, bk, out_
         for c in range(N_CHUNKS):
             xraw.append(xin.tile([P, 4 * D], U8, name="xraw%d" % c))
         nc.sync.dma_start(out=xraw[0][:], in_=x_view[0])
-        fraw = const.tile([P, 2, 4, 2, 128], BF16, name="fraw")
-        f_view = freqs.rearrange("(i p a) j e -> i p a (j e)", p=P, a=4)
-        for hh in range(2):
-            nc.sync.dma_start(out=fraw[:, 0, :, hh, :], in_=f_view[0])
         sc4 = const.tile([P, 4], F32, name="sc4")
         nc.sync.dma_start(out=sc4[:], in_=x_scale.rearrange("o n (p t) -> p (o n t)", t=4))
         wraw = const.tile([P, 2, 2, 2 * D], BF16, name="wraw")
         nc.sync.dma_start(out=wraw[:, 0], in_=wq.rearrange("(g m e) k -> m g (e k)", m=P, e=2))
         braw_q = const.tile([P, 2, 2], BF16, name="braw_q")
         nc.sync.dma_start(out=braw_q[:], in_=bq.rearrange("(g m e) -> m g e", m=P, e=2))
+        fraw = const.tile([P, 2, 4, 2, 128], BF16, name="fraw")
+        f_view = freqs.rearrange("(i p a) j e -> i p a (j e)", p=P, a=4)
+        for hh in range(2):
+            nc.sync.dma_start(out=fraw[:, 0, :, hh, :], in_=f_view[0])
+        nc.sync.dma_start(out=wraw[:, 1], in_=wk.rearrange("(g m e) k -> m g (e k)", m=P, e=2))
         braw_k = const.tile([P, 2, 2], BF16, name="braw_k")
         nc.sync.dma_start(out=braw_k[:], in_=bk.rearrange("(g m e) -> m g e", m=P, e=2))
-        nc.sync.dma_start(out=wraw[:, 1], in_=wk.rearrange("(g m e) k -> m g (e k)", m=P, e=2))
+        nc.sync.dma_start(out=xraw[1][:], in_=x_view[1])
         for hh in range(2):
             nc.sync.dma_start(out=fraw[:, 1, :, hh, :], in_=f_view[1])
-        for c in range(1, N_CHUNKS):
+        for c in range(2, N_CHUNKS):
             nc.sync.dma_start(out=xraw[c][:], in_=x_view[c])
 
         ident = const.tile([P, P], F32, name="ident")
@@ -65,21 +67,31 @@ def tile_attention_pa_t_kernel(tc, x_bytes, x_scale, freqs, wq, bq, wk, bk, out_
         ident_bf = const.tile([P, P], BF16, name="ident_bf")
         make_identity(nc, ident_bf[:])
 
-        bias = const.tile([P, 2, 2, 2], F32, name="bias")
-        for qk, braw in enumerate((braw_q, braw_k)):
-            nc.vector.tensor_copy(out=bias[:, qk], in_=braw[:])
-
-        sc_b = sc4[:].rearrange("p (o u e) -> p o u e", o=1, u=2).to_broadcast([P, 256, 2, 2])
         xstate = {}
+        sc_b = sc4[:].rearrange("p (o u e) -> p o u e", o=1, u=2).to_broadcast([P, 256, 2, 2])
+        sc_all = const.tile([P, 512], F32, name="sc_all")
 
-        def x_cast(c, h):
-            if h == 0:
+        def scales_spread():
+            sc_ps = ps_tp.tile([P, 4, P], F32, name="sc_ps", tag="tp")
+            for t in range(4):
+                nc.tensor.transpose(sc_ps[:, t, :], sc4[:, t : t + 1].to_broadcast([P, P]), ident[:])
+            nc.scalar.copy(
+                out=sc_all[:].rearrange("q (u p e) -> q u p e", u=2, e=2),
+                in_=sc_ps[:].rearrange("q (u e) p -> q u p e", u=2),
+            )
+
+        def x_cast(c, a0, n, eng):
+            if ("bf", c) not in xstate:
                 xstate[("bf", c)] = xw.tile([P, 4 * D], BF16, name="xbf")
-            cols = slice(h * 1024, (h + 1) * 1024)
-            nc.scalar.copy(out=xstate[("bf", c)][:, cols], in_=xraw[c][:, cols].bitcast(FP8))
+            cols = slice(a0 * D, (a0 + n) * D)
+            dst, src = xstate[("bf", c)][:, cols], xraw[c][:, cols].bitcast(FP8)
+            if eng == "v":
+                nc.vector.tensor_copy(out=dst, in_=src)
+            else:
+                nc.scalar.copy(out=dst, in_=src)
 
         def x_turn(c, h):
-            if h == 0:
+            if ("g", c) not in xstate:
                 xstate[("g", c)] = xw.tile([P, 4 * CHUNK], BF16, name="xg", align_bytes=64)
             words = xstate[("bf", c)][:].bitcast(F32)
             xt = ps_tp.tile([P, 2, 256], F32, name="xt", tag="tp")
@@ -89,11 +101,47 @@ def tile_attention_pa_t_kernel(tc, x_bytes, x_scale, freqs, wq, bq, wk, bk, out_
                     nc.tensor.transpose(
                         xt[:, u, aa * P : (aa + 1) * P], words[:, a * 256 + u : (a + 1) * 256 : 2], ident[:]
                     )
+            xstate[("xt", c, h)] = xt
+
+        def x_mul(c, h):
+            xt = xstate[("xt", c, h)]
             nc.vector.tensor_tensor(
                 out=xstate[("g", c)][:, h * 1024 : (h + 1) * 1024].rearrange("p (n u e) -> p n u e", u=2, e=2),
                 in0=xt[:].bitcast(BF16).rearrange("p u (n e) -> p n u e", e=2),
                 in1=sc_b,
                 op=ALU.mult,
+            )
+
+        def x_scale(c, h):
+            if ("sc", c) not in xstate:
+                xstate[("sc", c)] = xw.tile([P, 4 * D], BF16, name="xsc")
+            cols = slice(h * 1024, (h + 1) * 1024)
+            dst = xstate[("sc", c)][:, cols].rearrange("q (a u p e) -> q u a p e", a=2, u=2, e=2)
+            raw = xstate[("bf", c)][:, cols].rearrange("q (a p u e) -> q u a p e", a=2, u=2, e=2)
+            for u in range(2):
+                nc.gpsimd.tensor_tensor(
+                    out=dst[:, u],
+                    in0=raw[:, u],
+                    in1=sc_all[:, u * 256 : (u + 1) * 256]
+                    .rearrange("q (o p e) -> q o p e", o=1, e=2)
+                    .to_broadcast([P, 2, P, 2]),
+                    op=ALU.mult,
+                )
+
+        def x_turn_scaled(c, h):
+            if ("g", c) not in xstate:
+                xstate[("g", c)] = xw.tile([P, 4 * CHUNK], BF16, name="xg", align_bytes=64)
+            words = xstate[("sc", c)][:].bitcast(F32)
+            xt = ps_tp.tile([P, 2, 256], F32, name="xt", tag="tp")
+            for aa in range(2):
+                lo = (2 * h + aa) * 256
+                for u in range(2):
+                    nc.tensor.transpose(
+                        xt[:, u, aa * P : (aa + 1) * P], words[:, lo + u * P : lo + (u + 1) * P], ident[:]
+                    )
+            nc.scalar.copy(
+                out=xstate[("g", c)][:, h * 1024 : (h + 1) * 1024].bitcast(F32).rearrange("p (n u) -> p n u", u=2),
+                in_=xt[:].rearrange("p u n -> p n u"),
             )
 
         def x_quant(c):
@@ -106,40 +154,43 @@ def tile_attention_pa_t_kernel(tc, x_bytes, x_scale, freqs, wq, bq, wk, bk, out_
         wc = const.tile([P, 2 * 512], U32, name="wc", align_bytes=64)
         ws = const.tile([P, 2 * 512], U8, name="ws", align_bytes=64)
 
-        def w_prep(qk):
+        def w_turn(qk, g):
             words = wraw[:, qk].rearrange("p g f -> p (g f)").bitcast(F32)
-            for g in range(2):
-                wt = ps_tp.tile([P, 2, 256], F32, name="wt", tag="tp")
-                for e in range(2):
-                    ti = 2 * g + e
-                    for u in range(2):
-                        nc.tensor.transpose(
-                            wt[:, u, e * P : (e + 1) * P], words[:, ti * 256 + u : (ti + 1) * 256 : 2], ident[:]
-                        )
-                lo = qk * 2048 + g * 1024
-                nc.scalar.copy(
-                    out=wg[:, lo : lo + 1024].bitcast(F32).rearrange("p (n u) -> p n u", u=2),
-                    in_=wt[:].rearrange("p u n -> p n u"),
-                )
+            wt = ps_tp.tile([P, 2, 256], F32, name="wt", tag="tp")
+            for e in range(2):
+                ti = 2 * g + e
+                for u in range(2):
+                    nc.tensor.transpose(
+                        wt[:, u, e * P : (e + 1) * P], words[:, ti * 256 + u : (ti + 1) * 256 : 2], ident[:]
+                    )
+            lo = qk * 2048 + g * 1024
+            nc.scalar.copy(
+                out=wg[:, lo : lo + 1024].bitcast(F32).rearrange("p (n u) -> p n u", u=2),
+                in_=wt[:].rearrange("p u n -> p n u"),
+            )
+
+        def w_quant(qk, g):
+            lo = qk * 512 + g * 256
             nc.vector.quantize_mx(
-                out=wc[:, qk * 512 : (qk + 1) * 512].bitcast(FP8X4),
-                scales=ws[:, qk * 512 : (qk + 1) * 512],
-                in_=wg[:, qk * 2048 : (qk + 1) * 2048],
+                out=wc[:, lo : lo + 256].bitcast(FP8X4),
+                scales=ws[:, lo : lo + 256],
+                in_=wg[:, 4 * lo : 4 * lo + 1024],
             )
 
         tabs = const.tile([P, 2, 3, CHUNK], F32, name="tabs")
         fr = fraw[:].rearrange("p i a hh (j e) -> p i a (hh j) e", e=2)
 
-        def tables_turn(i):
-            for e in (0, 1):
-                tt = ps_tp.tile([P, CHUNK], BF16, name="tt", tag="tp")
-                for a in range(4):
-                    nc.tensor.transpose(tt[:, a * P : (a + 1) * P], fr[:, i, a, :, e], ident_bf[:])
-                if e == 0:
-                    nc.scalar.activation(out=tabs[:, i, 1, :], in_=tt[:], func=ACT.Copy, scale=1.0)
-                else:
-                    nc.scalar.activation(out=tabs[:, i, 2, :], in_=tt[:], func=ACT.Copy, scale=-1.0)
-                    nc.scalar.activation(out=tabs[:, i, 0, :], in_=tt[:], func=ACT.Copy, scale=1.0)
+        def tables_turn(i, e):
+            tt = ps_tp.tile([P, CHUNK], BF16, name="tt", tag="tp")
+            for a in range(4):
+                nc.tensor.transpose(tt[:, a * P : (a + 1) * P], fr[:, i, a, :, e], ident_bf[:])
+            if e == 0:
+                nc.scalar.activation(out=tabs[:, i, 1, :], in_=tt[:], func=ACT.Copy, scale=1.0)
+            else:
+                nc.scalar.activation(out=tabs[:, i, 2, :], in_=tt[:], func=ACT.Copy, scale=-1.0)
+                nc.scalar.activation(out=tabs[:, i, 0, :], in_=tt[:], func=ACT.Copy, scale=1.0)
+
+        bias = const.tile([P, 2, 2, 2], F32, name="bias")
 
         steps = [(c, qk, g) for c in range(N_CHUNKS) for qk in range(2) for g in range(2)]
         n_steps = len(steps)
@@ -147,7 +198,7 @@ def tile_attention_pa_t_kernel(tc, x_bytes, x_scale, freqs, wq, bq, wk, bk, out_
         otiles = {}
 
         def v_takes(n):
-            return (n % 2 == 1 and n % 8 != 3) or n >= n_steps - 2
+            return (n % 3 != 2) or n >= n_steps - 2
 
         def front_mx(n):
             c, qk, g = steps[n]
@@ -173,6 +224,7 @@ def tile_attention_pa_t_kernel(tc, x_bytes, x_scale, freqs, wq, bq, wk, bk, out_
             c, qk, g = steps[n]
             i = c % 2
             xb, xa = live[("x", n)]
+
             def vpair(acc, e, slots, nm):
                 k = work.tile([P, 2, CHUNK], F32, name=nm)
                 nc.vector.scalar_tensor_tensor(
@@ -185,7 +237,6 @@ def tile_attention_pa_t_kernel(tc, x_bytes, x_scale, freqs, wq, bq, wk, bk, out_
                 )
                 return k
 
-            re = None
             if v_takes(n):
                 vb = vpair(xb, 1, slice(1, 3), "vb")
                 ga = vpair(xa, 0, slice(0, 2), "ga")
@@ -194,12 +245,13 @@ def tile_attention_pa_t_kernel(tc, x_bytes, x_scale, freqs, wq, bq, wk, bk, out_
                 nc.scalar.activation(out=a1[:], in_=xa[:], func=ACT.Identity, bias=bias[:, qk, g, 0:1], scale=1.0)
                 vb = vpair(xb, 1, slice(1, 3), "vb")
                 ga = work.tile([P, 2, CHUNK], F32, name="ga")
-                for slot in (1, 0):
-                    nc.gpsimd.tensor_tensor(out=ga[:, slot, :], in0=a1[:], in1=tabs[:, i, slot, :], op=ALU.mult)
-            live[("k", n)] = (
-                (ga[:, 1, :], vb[:, 1, :]) if re is None else (re[:],),
-                (ga[:, 0, :], vb[:, 0, :]),
-            )
+                nc.gpsimd.tensor_tensor(
+                    out=ga[:],
+                    in0=a1[:].rearrange("p (o n) -> p o n", o=1).to_broadcast([P, 2, CHUNK]),
+                    in1=tabs[:, i, 0:2, :],
+                    op=ALU.mult,
+                )
+            live[("k", n)] = ((ga[:, 1, :], vb[:, 1, :]), (ga[:, 0, :], vb[:, 0, :]))
 
         def back(n):
             c, qk, g = steps[n]
@@ -236,35 +288,57 @@ def tile_attention_pa_t_kernel(tc, x_bytes, x_scale, freqs, wq, bq, wk, bk, out_
             elif g == 1:
                 nc.sync.dma_start(out=o_views[qk][c], in_=o[:].rearrange("p a f -> p (a f)"))
 
-        x_cast(0, 0)
-        x_cast(0, 1)
-        tables_turn(0)
+        x_cast(0, 0, 2, "v")
+        x_cast(0, 2, 2, "s")
         x_turn(0, 0)
+        x_mul(0, 0)
+        w_turn(0, 0)
         x_turn(0, 1)
-        w_prep(0)
+        w_turn(0, 1)
+        w_quant(0, 0)
+        x_mul(0, 1)
+        tables_turn(0, 0)
         x_quant(0)
-        tables_turn(1)
-        w_prep(1)
-        x_cast(1, 0)
-        x_cast(1, 1)
-        x_turn(1, 0)
-
+        nc.vector.tensor_copy(out=bias[:, 0], in_=braw_q[:])
+        nc.vector.tensor_copy(out=bias[:, 1], in_=braw_k[:])
+        tables_turn(0, 1)
+        w_quant(0, 1)
+        x_cast(1, 0, 4, "v")
         n_halves = 2 * N_CHUNKS
-        with tc.manual_schedule(engines={mybir.EngineType.PE}):
-            for k in range((n_steps + LAG + 1) // 2):
-                pair = (2 * k, 2 * k + 1)
-                for n in pair:
-                    if n < n_steps:
-                        front_mx(n)
-                if k % 2 == 1 and (k + 1) // 2 < N_CHUNKS:
-                    x_quant((k + 1) // 2)
-                for n in pair:
-                    if n < n_steps:
-                        front_mul(n)
-                for n in pair:
-                    if LAG <= n < n_steps + LAG:
-                        back(n - LAG)
-                if k + 3 < n_halves:
-                    x_turn((k + 3) // 2, (k + 3) % 2)
-                if k + 4 < n_halves:
-                    x_cast((k + 4) // 2, (k + 4) % 2)
+        for k in range((n_steps + LAG + 1) // 2):
+            pair = (2 * k, 2 * k + 1)
+            for n in pair:
+                if n < n_steps:
+                    front_mx(n)
+            if k == 0:
+                w_turn(1, 0)
+                w_turn(1, 1)
+                x_turn(1, 0)
+            if k % 2 == 1 and (k + 1) // 2 < N_CHUNKS and k > 0:
+                x_quant((k + 1) // 2)
+            for n in pair:
+                if n < n_steps:
+                    front_mul(n)
+                if n == 0:
+                    w_quant(1, 0)
+                    w_quant(1, 1)
+                    scales_spread()
+                    x_cast(2, 0, 4, "s")
+                    x_mul(1, 0)
+            for n in pair:
+                if LAG <= n < n_steps + LAG:
+                    back(n - LAG)
+            if k == 0:
+                x_turn(1, 1)
+                x_mul(1, 1)
+                x_scale(2, 0)
+                x_scale(2, 1)
+                x_cast(3, 0, 2, "s")
+                tables_turn(1, 0)
+                tables_turn(1, 1)
+            if 4 <= k + 3 < n_halves:
+                x_turn_scaled((k + 3) // 2, (k + 3) % 2)
+            if 6 <= k + 4 < n_halves:
+                x_scale((k + 4) // 2, (k + 4) % 2)
+            if 7 <= k + 6 < n_halves:
+                x_cast((k + 6) // 2, 2 * ((k + 6) % 2), 2, "s")

@@ -18,7 +18,7 @@ FLOPS = 2 * B * S * D * 2 * D
 P = 128
 CHUNK = 512
 N_CHUNKS = B * S // CHUNK
-LAG = 3
+LAG = 2
 
 
 def tile_attention_pa_t_kernel(tc, x_bytes, x_scale, freqs, wq, bq, wk, bk, out_q, out_k):
@@ -28,6 +28,7 @@ def tile_attention_pa_t_kernel(tc, x_bytes, x_scale, freqs, wq, bq, wk, bk, out_
         const = ctx.enter_context(tc.tile_pool(name="const", bufs=1))
         xin = ctx.enter_context(tc.tile_pool(name="xin", bufs=1))
         xw = ctx.enter_context(tc.tile_pool(name="xw", bufs=3))
+        xring = ctx.enter_context(tc.tile_pool(name="xring", bufs=4))
         work = ctx.enter_context(tc.tile_pool(name="work", bufs=6))
         outp = ctx.enter_context(tc.tile_pool(name="outp", bufs=3))
         ps_mx = ctx.enter_context(tc.psum_pool(name="ps_mx", bufs=5))
@@ -92,7 +93,7 @@ def tile_attention_pa_t_kernel(tc, x_bytes, x_scale, freqs, wq, bq, wk, bk, out_
 
         def x_turn(c, h):
             if ("g", c) not in xstate:
-                xstate[("g", c)] = xw.tile([P, 4 * CHUNK], BF16, name="xg", align_bytes=64)
+                xstate[("g", c)] = xring.tile([P, 4 * CHUNK], BF16, name="xg", tag="ring", align_bytes=64)
             words = xstate[("bf", c)][:].bitcast(F32)
             xt = ps_tp.tile([P, 2, 256], F32, name="xt", tag="tp")
             for aa in range(2):
@@ -113,10 +114,10 @@ def tile_attention_pa_t_kernel(tc, x_bytes, x_scale, freqs, wq, bq, wk, bk, out_
             )
 
         def x_scale(c, h):
-            if ("sc", c) not in xstate:
-                xstate[("sc", c)] = xw.tile([P, 4 * D], BF16, name="xsc")
             cols = slice(h * 1024, (h + 1) * 1024)
-            dst = xstate[("sc", c)][:, cols].rearrange("q (a u p e) -> q u a p e", a=2, u=2, e=2)
+            xsc = xring.tile([P, 2 * D], BF16, name="xsc", tag="ring", align_bytes=64)
+            xstate[("sc", c, h)] = xsc
+            dst = xsc[:].rearrange("q (a u p e) -> q u a p e", a=2, u=2, e=2)
             raw = xstate[("bf", c)][:, cols].rearrange("q (a p u e) -> q u a p e", a=2, u=2, e=2)
             for u in range(2):
                 nc.gpsimd.tensor_tensor(
@@ -130,11 +131,11 @@ def tile_attention_pa_t_kernel(tc, x_bytes, x_scale, freqs, wq, bq, wk, bk, out_
 
         def x_turn_scaled(c, h):
             if ("g", c) not in xstate:
-                xstate[("g", c)] = xw.tile([P, 4 * CHUNK], BF16, name="xg", align_bytes=64)
-            words = xstate[("sc", c)][:].bitcast(F32)
+                xstate[("g", c)] = xring.tile([P, 4 * CHUNK], BF16, name="xg", tag="ring", align_bytes=64)
+            words = xstate[("sc", c, h)][:].bitcast(F32)
             xt = ps_tp.tile([P, 2, 256], F32, name="xt", tag="tp")
             for aa in range(2):
-                lo = (2 * h + aa) * 256
+                lo = aa * 256
                 for u in range(2):
                     nc.tensor.transpose(
                         xt[:, u, aa * P : (aa + 1) * P], words[:, lo + u * P : lo + (u + 1) * P], ident[:]
@@ -198,7 +199,7 @@ def tile_attention_pa_t_kernel(tc, x_bytes, x_scale, freqs, wq, bq, wk, bk, out_
         otiles = {}
 
         def v_takes(n):
-            return (n % 3 != 2) or n >= n_steps - 2
+            return (n % 4 != 0) or n >= n_steps - 2
 
         def front_mx(n):
             c, qk, g = steps[n]
@@ -314,11 +315,11 @@ def tile_attention_pa_t_kernel(tc, x_bytes, x_scale, freqs, wq, bq, wk, bk, out_
                 w_turn(1, 0)
                 w_turn(1, 1)
                 x_turn(1, 0)
-            if k % 2 == 1 and (k + 1) // 2 < N_CHUNKS and k > 0:
-                x_quant((k + 1) // 2)
             for n in pair:
                 if n < n_steps:
                     front_mul(n)
+                if n % 4 == 2 and n // 4 + 1 < N_CHUNKS:
+                    x_quant(n // 4 + 1)
                 if n == 0:
                     w_quant(1, 0)
                     w_quant(1, 1)
@@ -332,13 +333,12 @@ def tile_attention_pa_t_kernel(tc, x_bytes, x_scale, freqs, wq, bq, wk, bk, out_
                 x_turn(1, 1)
                 x_mul(1, 1)
                 x_scale(2, 0)
-                x_scale(2, 1)
                 x_cast(3, 0, 2, "s")
                 tables_turn(1, 0)
                 tables_turn(1, 1)
             if 4 <= k + 3 < n_halves:
                 x_turn_scaled((k + 3) // 2, (k + 3) % 2)
-            if 6 <= k + 4 < n_halves:
+            if 5 <= k + 4 < n_halves:
                 x_scale((k + 4) // 2, (k + 4) % 2)
             if 7 <= k + 6 < n_halves:
                 x_cast((k + 6) // 2, 2 * ((k + 6) % 2), 2, "s")

@@ -28,7 +28,7 @@ def tile_attention_pa_t_kernel(tc, x_bytes, x_scale, freqs, wq, bq, wk, bk, out_
         const = ctx.enter_context(tc.tile_pool(name="const", bufs=1))
         xin = ctx.enter_context(tc.tile_pool(name="xin", bufs=1))
         xw = ctx.enter_context(tc.tile_pool(name="xw", bufs=3))
-        xring = ctx.enter_context(tc.tile_pool(name="xring", bufs=4))
+        xring = ctx.enter_context(tc.tile_pool(name="xring", bufs=3))
         work = ctx.enter_context(tc.tile_pool(name="work", bufs=6))
         outp = ctx.enter_context(tc.tile_pool(name="outp", bufs=3))
         ps_mx = ctx.enter_context(tc.psum_pool(name="ps_mx", bufs=5))
@@ -113,29 +113,25 @@ def tile_attention_pa_t_kernel(tc, x_bytes, x_scale, freqs, wq, bq, wk, bk, out_
                 op=ALU.mult,
             )
 
-        def x_scale(c, h):
-            cols = slice(h * 1024, (h + 1) * 1024)
-            xsc = xring.tile([P, 2 * D], BF16, name="xsc", tag="ring", align_bytes=64)
-            xstate[("sc", c, h)] = xsc
-            dst = xsc[:].rearrange("q (a u p e) -> q u a p e", a=2, u=2, e=2)
-            raw = xstate[("bf", c)][:, cols].rearrange("q (a p u e) -> q u a p e", a=2, u=2, e=2)
-            for u in range(2):
-                nc.gpsimd.tensor_tensor(
-                    out=dst[:, u],
-                    in0=raw[:, u],
-                    in1=sc_all[:, u * 256 : (u + 1) * 256]
-                    .rearrange("q (o p e) -> q o p e", o=1, e=2)
-                    .to_broadcast([P, 2, P, 2]),
-                    op=ALU.mult,
-                )
+        def x_scale(c, u):
+            if u == 0:
+                xstate[("sc", c)] = xring.tile([P, 4 * D], BF16, name="xsc", tag="ring", align_bytes=64)
+            nc.gpsimd.tensor_tensor(
+                out=xstate[("sc", c)][:].rearrange("q (a u p e) -> q u a p e", a=4, u=2, e=2)[:, u],
+                in0=xstate[("bf", c)][:].rearrange("q (a p u e) -> q u a p e", a=4, u=2, e=2)[:, u],
+                in1=sc_all[:, u * 256 : (u + 1) * 256]
+                .rearrange("q (o p e) -> q o p e", o=1, e=2)
+                .to_broadcast([P, 4, P, 2]),
+                op=ALU.mult,
+            )
 
         def x_turn_scaled(c, h):
             if ("g", c) not in xstate:
                 xstate[("g", c)] = xring.tile([P, 4 * CHUNK], BF16, name="xg", tag="ring", align_bytes=64)
-            words = xstate[("sc", c, h)][:].bitcast(F32)
+            words = xstate[("sc", c)][:].bitcast(F32)
             xt = ps_tp.tile([P, 2, 256], F32, name="xt", tag="tp")
             for aa in range(2):
-                lo = aa * 256
+                lo = (2 * h + aa) * 256
                 for u in range(2):
                     nc.tensor.transpose(
                         xt[:, u, aa * P : (aa + 1) * P], words[:, lo + u * P : lo + (u + 1) * P], ident[:]
@@ -333,12 +329,15 @@ def tile_attention_pa_t_kernel(tc, x_bytes, x_scale, freqs, wq, bq, wk, bk, out_
                 x_turn(1, 1)
                 x_mul(1, 1)
                 x_scale(2, 0)
+                x_scale(2, 1)
                 x_cast(3, 0, 2, "s")
                 tables_turn(1, 0)
                 tables_turn(1, 1)
             if 4 <= k + 3 < n_halves:
                 x_turn_scaled((k + 3) // 2, (k + 3) % 2)
-            if 5 <= k + 4 < n_halves:
-                x_scale((k + 4) // 2, (k + 4) % 2)
-            if 7 <= k + 6 < n_halves:
-                x_cast((k + 6) // 2, 2 * ((k + 6) % 2), 2, "s")
+            if 6 <= k + 5 < n_halves:
+                x_scale((k + 5) // 2, (k + 5) % 2)
+            if k == 0:
+                x_cast(3, 2, 2, "s")
+            if 8 <= k + 7 < n_halves:
+                x_cast((k + 7) // 2, 2 * ((k + 7) % 2), 2, "s")

@@ -113,15 +113,16 @@ def tile_attention_pa_t_kernel(tc, x_bytes, x_scale, freqs, wq, bq, wk, bk, out_
                 op=ALU.mult,
             )
 
-        def x_scale(c, u):
-            if u == 0:
+        def x_scale(c, u, a0=0, n=4):
+            if ("sc", c) not in xstate:
                 xstate[("sc", c)] = xring.tile([P, 4 * D], BF16, name="xsc", tag="ring", align_bytes=64)
+            cols = slice(a0 * D, (a0 + n) * D)
             nc.gpsimd.tensor_tensor(
-                out=xstate[("sc", c)][:].rearrange("q (a u p e) -> q u a p e", a=4, u=2, e=2)[:, u],
-                in0=xstate[("bf", c)][:].rearrange("q (a p u e) -> q u a p e", a=4, u=2, e=2)[:, u],
+                out=xstate[("sc", c)][:, cols].rearrange("q (a u p e) -> q u a p e", a=n, u=2, e=2)[:, u],
+                in0=xstate[("bf", c)][:, cols].rearrange("q (a p u e) -> q u a p e", a=n, u=2, e=2)[:, u],
                 in1=sc_all[:, u * 256 : (u + 1) * 256]
                 .rearrange("q (o p e) -> q o p e", o=1, e=2)
-                .to_broadcast([P, 4, P, 2]),
+                .to_broadcast([P, n, P, 2]),
                 op=ALU.mult,
             )
 
@@ -248,7 +249,7 @@ def tile_attention_pa_t_kernel(tc, x_bytes, x_scale, freqs, wq, bq, wk, bk, out_
                     in1=tabs[:, i, 0:2, :],
                     op=ALU.mult,
                 )
-            live[("k", n)] = ((ga[:, 1, :], vb[:, 1, :]), (ga[:, 0, :], vb[:, 0, :]))
+            live[("k", n)] = [(ga[:, 1, :], vb[:, 1, :]), (ga[:, 0, :], vb[:, 0, :])]
 
         def back(n):
             c, qk, g = steps[n]
@@ -256,6 +257,36 @@ def tile_attention_pa_t_kernel(tc, x_bytes, x_scale, freqs, wq, bq, wk, bk, out_
                 otiles[(c, qk)] = outp.tile([P, 4, D], F32, name="o")
             o = otiles[(c, qk)]
             ov = o[:].rearrange("p a (g hh half j) -> p a g hh half j", g=2, hh=2, half=2)
+            if n == n_steps - 1:
+                for ap in range(2):
+                    tp = ps_tp.tile([P, CHUNK], F32, name="bt", tag="tp")
+                    for al in range(2):
+                        for half in range(2):
+                            a = 2 * ap + al
+                            blk = slice(a * P, (a + 1) * P)
+                            terms = live[("k", n)][half]
+                            lo = (2 * al + half) * P
+                            for ti, t in enumerate(terms):
+                                nc.tensor.matmul(
+                                    out=tp[:, lo : lo + P],
+                                    lhsT=t[:, blk],
+                                    rhs=ident[:],
+                                    is_transpose=True,
+                                    start=(ti == 0),
+                                    stop=(ti == len(terms) - 1),
+                                )
+                    dst = ov[:, 2 * ap : 2 * ap + 2, g]
+                    for half in range(2):
+                        srcv = tp[:].rearrange("p (a half hh j) -> p a half hh j", a=2, half=2, hh=2)[:, :, half]
+                        if half == 0:
+                            nc.scalar.copy(out=dst[:, :, :, half, :], in_=srcv)
+                        else:
+                            nc.vector.tensor_copy(out=dst[:, :, :, half, :], in_=srcv)
+                    nc.sync.dma_start(
+                        out=o_views[qk][c].rearrange("p (a g f) -> p a g f", a=4, g=2)[:, 2 * ap : 2 * ap + 2, g, :],
+                        in_=o[:].rearrange("p a (g f) -> p a g f", g=2)[:, 2 * ap : 2 * ap + 2, g, :],
+                    )
+                return
             last = n >= n_steps - 2
             for half in range(2):
                 tp = ps_tp.tile([P, CHUNK], F32, name="bt", tag="tp")
@@ -277,7 +308,7 @@ def tile_attention_pa_t_kernel(tc, x_bytes, x_scale, freqs, wq, bq, wk, bk, out_
                     nc.vector.tensor_copy(out=dst, in_=srcv)
                 else:
                     nc.scalar.copy(out=dst, in_=srcv)
-            if last:
+            if n >= n_steps - 4:
                 nc.sync.dma_start(
                     out=o_views[qk][c].rearrange("p (a g f) -> p a g f", a=4, g=2)[:, :, g, :],
                     in_=o[:].rearrange("p a (g f) -> p a g f", g=2)[:, :, g, :],
@@ -325,6 +356,8 @@ def tile_attention_pa_t_kernel(tc, x_bytes, x_scale, freqs, wq, bq, wk, bk, out_
             for n in pair:
                 if LAG <= n < n_steps + LAG:
                     back(n - LAG)
+                if n % 2 == 0 and 8 <= k + 7 < n_halves:
+                    x_cast((k + 7) // 2, 2 * ((k + 7) % 2), 2, "s")
             if k == 0:
                 x_turn(1, 1)
                 x_mul(1, 1)
@@ -339,5 +372,3 @@ def tile_attention_pa_t_kernel(tc, x_bytes, x_scale, freqs, wq, bq, wk, bk, out_
                 x_scale((k + 5) // 2, (k + 5) % 2)
             if k == 0:
                 x_cast(3, 2, 2, "s")
-            if 8 <= k + 7 < n_halves:
-                x_cast((k + 7) // 2, 2 * ((k + 7) % 2), 2, "s")

@@ -196,7 +196,7 @@ def tile_attention_pa_t_kernel(tc, x_bytes, x_scale, freqs, wq, bq, wk, bk, out_
         otiles = {}
 
         def v_takes(n):
-            return (n % 4 != 0) or n >= n_steps - 2
+            return n % 4 != 0
 
         def front_mx(n):
             c, qk, g = steps[n]
@@ -250,6 +250,12 @@ def tile_attention_pa_t_kernel(tc, x_bytes, x_scale, freqs, wq, bq, wk, bk, out_
                     op=ALU.mult,
                 )
             live[("k", n)] = [(ga[:, 1, :], vb[:, 1, :]), (ga[:, 0, :], vb[:, 0, :])]
+
+        def add_up(n, half):
+            a, b = live[("k", n)][half]
+            s = work.tile([P, CHUNK], F32, name="s%d" % half)
+            nc.gpsimd.tensor_tensor(out=s[:], in0=a, in1=b, op=ALU.add)
+            live[("k", n)][half] = (s[:],)
 
         def back(n):
             c, qk, g = steps[n]
@@ -330,6 +336,7 @@ def tile_attention_pa_t_kernel(tc, x_bytes, x_scale, freqs, wq, bq, wk, bk, out_
         nc.vector.tensor_copy(out=bias[:, 0], in_=braw_q[:])
         nc.vector.tensor_copy(out=bias[:, 1], in_=braw_k[:])
         tables_turn(0, 1)
+        scales_spread()
         w_quant(0, 1)
         x_cast(1, 0, 4, "v")
         n_halves = 2 * N_CHUNKS
@@ -350,9 +357,12 @@ def tile_attention_pa_t_kernel(tc, x_bytes, x_scale, freqs, wq, bq, wk, bk, out_
                 if n == 0:
                     w_quant(1, 0)
                     w_quant(1, 1)
-                    scales_spread()
                     x_cast(2, 0, 4, "s")
                     x_mul(1, 0)
+            if 11 <= k < 15:
+                if v_takes(2 * k):
+                    add_up(2 * k, 0)
+                add_up(2 * k + 1, 1)
             for n in pair:
                 if LAG <= n < n_steps + LAG:
                     back(n - LAG)

from contextlib import ExitStack

import concourse.mybir as mybir
from concourse.masks import make_identity

F32 = mybir.dt.float32
BF16 = mybir.dt.bfloat16
U8 = mybir.dt.uint8
U32 = mybir.dt.uint32
FP8 = mybir.dt.float8_e4m3fn
FP8X4 = mybir.dt.float8_e4m3fn_x4
ALU = mybir.AluOpType
ACT = mybir.ActivationFunctionType

B, S, D, H = 4, 1024, 512, 4
FLOPS = 2 * B * S * D * 2 * D

P = 128
CHUNK = 512
N_CHUNKS = B * S // CHUNK
LAG = 2


def tile_attention_pa_t_kernel(tc, x_bytes, x_scale, freqs, wq, bq, wk, bk, out_q, out_k):
    nc = tc.nc
    with ExitStack() as ctx:
        ctx.enter_context(tc.manual_schedule())
        const = ctx.enter_context(tc.tile_pool(name="const", bufs=1))
        xin = ctx.enter_context(tc.tile_pool(name="xin", bufs=1))
        xw = ctx.enter_context(tc.tile_pool(name="xw", bufs=3))
        xring = ctx.enter_context(tc.tile_pool(name="xring", bufs=3))
        work = ctx.enter_context(tc.tile_pool(name="work", bufs=6))
        outp = ctx.enter_context(tc.tile_pool(name="outp", bufs=3))
        ps_mx = ctx.enter_context(tc.psum_pool(name="ps_mx", bufs=5))
        ps_tp = ctx.enter_context(tc.psum_pool(name="ps_tp", bufs=3))

        x_view = x_bytes.rearrange("b s k -> (b s) k").rearrange("(c p a) k -> c p (a k)", p=P, a=4)
        o_views = [
            o.rearrange("b s h d -> (b s) (h d)").rearrange("(c p a) f -> c p (a f)", p=P, a=4)
            for o in (out_q, out_k)
        ]

        xraw = []
        for c in range(N_CHUNKS):
            xraw.append(xin.tile([P, 4 * D], U8, name="xraw%d" % c))
        nc.sync.dma_start(out=xraw[0][:], in_=x_view[0])
        sc4 = const.tile([P, 4], F32, name="sc4")
        nc.sync.dma_start(out=sc4[:], in_=x_scale.rearrange("o n (p t) -> p (o n t)", t=4))
        wraw = const.tile([P, 2, 2, 2 * D], BF16, name="wraw")
        nc.sync.dma_start(out=wraw[:, 0], in_=wq.rearrange("(g m e) k -> m g (e k)", m=P, e=2))
        braw_q = const.tile([P, 2, 2], BF16, name="braw_q")
        nc.sync.dma_start(out=braw_q[:], in_=bq.rearrange("(g m e) -> m g e", m=P, e=2))
        fraw = const.tile([P, 2, 4, 2, 128], BF16, name="fraw")
        f_view = freqs.rearrange("(i p a) j e -> i p a (j e)", p=P, a=4)
        for hh in range(2):
            nc.sync.dma_start(out=fraw[:, 0, :, hh, :], in_=f_view[0])
        nc.sync.dma_start(out=wraw[:, 1], in_=wk.rearrange("(g m e) k -> m g (e k)", m=P, e=2))
        braw_k = const.tile([P, 2, 2], BF16, name="braw_k")
        nc.sync.dma_start(out=braw_k[:], in_=bk.rearrange("(g m e) -> m g e", m=P, e=2))
        nc.sync.dma_start(out=xraw[1][:], in_=x_view[1])
        for hh in range(2):
            nc.sync.dma_start(out=fraw[:, 1, :, hh, :], in_=f_view[1])
        for c in range(2, N_CHUNKS):
            nc.sync.dma_start(out=xraw[c][:], in_=x_view[c])

        ident = const.tile([P, P], F32, name="ident")
        make_identity(nc, ident[:])
        ident_bf = const.tile([P, P], BF16, name="ident_bf")
        make_identity(nc, ident_bf[:])

        xstate = {}
        sc_b = sc4[:].rearrange("p (o u e) -> p o u e", o=1, u=2).to_broadcast([P, 256, 2, 2])
        sc_all = const.tile([P, 512], F32, name="sc_all")

        def scales_spread():
            sc_ps = ps_tp.tile([P, 4, P], F32, name="sc_ps", tag="tp")
            for t in range(4):
                nc.tensor.transpose(sc_ps[:, t, :], sc4[:, t : t + 1].to_broadcast([P, P]), ident[:])
            nc.scalar.copy(
                out=sc_all[:].rearrange("q (u p e) -> q u p e", u=2, e=2),
                in_=sc_ps[:].rearrange("q (u e) p -> q u p e", u=2),
            )

        def x_cast(c, a0, n, eng):
            if ("bf", c) not in xstate:
                xstate[("bf", c)] = xw.tile([P, 4 * D], BF16, name="xbf")
            cols = slice(a0 * D, (a0 + n) * D)
            dst, src = xstate[("bf", c)][:, cols], xraw[c][:, cols].bitcast(FP8)
            if eng == "v":
                nc.vector.tensor_copy(out=dst, in_=src)
            else:
                nc.scalar.copy(out=dst, in_=src)

        def x_turn(c, h):
            if ("g", c) not in xstate:
                xstate[("g", c)] = xring.tile([P, 4 * CHUNK], BF16, name="xg", tag="ring", align_bytes=64)
            words = xstate[("bf", c)][:].bitcast(F32)
            xt = ps_tp.tile([P, 2, 256], F32, name="xt", tag="tp")
            for aa in range(2):
                a = 2 * h + aa
                for u in range(2):
                    nc.tensor.transpose(
                        xt[:, u, aa * P : (aa + 1) * P], words[:, a * 256 + u : (a + 1) * 256 : 2], ident[:]
                    )
            xstate[("xt", c, h)] = xt

        def x_mul(c, h):
            xt = xstate[("xt", c, h)]
            nc.vector.tensor_tensor(
                out=xstate[("g", c)][:, h * 1024 : (h + 1) * 1024].rearrange("p (n u e) -> p n u e", u=2, e=2),
                in0=xt[:].bitcast(BF16).rearrange("p u (n e) -> p n u e", e=2),
                in1=sc_b,
                op=ALU.mult,
            )

        def x_scale(c, u, a0=0, n=4):
            if ("sc", c) not in xstate:
                xstate[("sc", c)] = xring.tile([P, 4 * D], BF16, name="xsc", tag="ring", align_bytes=64)
            cols = slice(a0 * D, (a0 + n) * D)
            nc.gpsimd.tensor_tensor(
                out=xstate[("sc", c)][:, cols].rearrange("q (a u p e) -> q u a p e", a=n, u=2, e=2)[:, u],
                in0=xstate[("bf", c)][:, cols].rearrange("q (a p u e) -> q u a p e", a=n, u=2, e=2)[:, u],
                in1=sc_all[:, u * 256 : (u + 1) * 256]
                .rearrange("q (o p e) -> q o p e", o=1, e=2)
                .to_broadcast([P, n, P, 2]),
                op=ALU.mult,
            )

        def x_turn_scaled(c, h):
            if ("g", c) not in xstate:
                xstate[("g", c)] = xring.tile([P, 4 * CHUNK], BF16, name="xg", tag="ring", align_bytes=64)
            words = xstate[("sc", c)][:].bitcast(F32)
            xt = ps_tp.tile([P, 2, 256], F32, name="xt", tag="tp")
            for aa in range(2):
                lo = (2 * h + aa) * 256
                for u in range(2):
                    nc.tensor.transpose(
                        xt[:, u, aa * P : (aa + 1) * P], words[:, lo + u * P : lo + (u + 1) * P], ident[:]
                    )
            nc.scalar.copy(
                out=xstate[("g", c)][:, h * 1024 : (h + 1) * 1024].bitcast(F32).rearrange("p (n u) -> p n u", u=2),
                in_=xt[:].rearrange("p u n -> p n u"),
            )

        def x_quant(c):
            xc = xw.tile([P, CHUNK], U32, name="xc", align_bytes=64)
            xs = xw.tile([P, CHUNK], U8, name="xs", align_bytes=64)
            nc.vector.quantize_mx(out=xc[:].bitcast(FP8X4), scales=xs[:], in_=xstate[("g", c)][:])
            xstate[("q", c)] = (xc, xs)

        wg = const.tile([P, 2 * 2048], BF16, name="wg", align_bytes=64)
        wc = const.tile([P, 2 * 512], U32, name="wc", align_bytes=64)
        ws = const.tile([P, 2 * 512], U8, name="ws", align_bytes=64)

        def w_turn(qk, g):
            words = wraw[:, qk].rearrange("p g f -> p (g f)").bitcast(F32)
            wt = ps_tp.tile([P, 2, 256], F32, name="wt", tag="tp")
            for e in range(2):
                ti = 2 * g + e
                for u in range(2):
                    nc.tensor.transpose(
                        wt[:, u, e * P : (e + 1) * P], words[:, ti * 256 + u : (ti + 1) * 256 : 2], ident[:]
                    )
            lo = qk * 2048 + g * 1024
            nc.scalar.copy(
                out=wg[:, lo : lo + 1024].bitcast(F32).rearrange("p (n u) -> p n u", u=2),
                in_=wt[:].rearrange("p u n -> p n u"),
            )

        def w_quant(qk, g):
            lo = qk * 512 + g * 256
            nc.vector.quantize_mx(
                out=wc[:, lo : lo + 256].bitcast(FP8X4),
                scales=ws[:, lo : lo + 256],
                in_=wg[:, 4 * lo : 4 * lo + 1024],
            )

        tabs = const.tile([P, 2, 3, CHUNK], F32, name="tabs")
        fr = fraw[:].rearrange("p i a hh (j e) -> p i a (hh j) e", e=2)

        def tables_turn(i, e):
            tt = ps_tp.tile([P, CHUNK], BF16, name="tt", tag="tp")
            for a in range(4):
                nc.tensor.transpose(tt[:, a * P : (a + 1) * P], fr[:, i, a, :, e], ident_bf[:])
            if e == 0:
                nc.scalar.activation(out=tabs[:, i, 1, :], in_=tt[:], func=ACT.Copy, scale=1.0)
            else:
                nc.scalar.activation(out=tabs[:, i, 2, :], in_=tt[:], func=ACT.Copy, scale=-1.0)
                nc.scalar.activation(out=tabs[:, i, 0, :], in_=tt[:], func=ACT.Copy, scale=1.0)

        bias = const.tile([P, 2, 2, 2], F32, name="bias")

        steps = [(c, qk, g) for c in range(N_CHUNKS) for qk in range(2) for g in range(2)]
        n_steps = len(steps)
        live = {}
        otiles = {}

        def v_takes(n):
            return n % 4 != 0

        def front_mx(n):
            c, qk, g = steps[n]
            xc, xs = xstate[("q", c)]
            base = qk * 512 + g * 256
            accs = []
            for e, nm in ((1, "xb"), (0, "xa")):
                cols = slice(base + e * P, base + (e + 1) * P)
                acc = ps_mx.tile([P, CHUNK], F32, name=nm, tag="mx")
                nc.tensor.matmul_mx(
                    out=acc[:],
                    lhsT=wc[:, cols].bitcast(FP8X4),
                    lhsT_scale=ws[:, cols],
                    rhs=xc[:].bitcast(FP8X4),
                    rhs_scale=xs[:],
                    start=True,
                    stop=True,
                )
                accs.append(acc)
            live[("x", n)] = accs

        def front_mul(n):
            c, qk, g = steps[n]
            i = c % 2
            xb, xa = live[("x", n)]

            def vpair(acc, e, slots, nm):
                k = work.tile([P, 2, CHUNK], F32, name=nm)
                nc.vector.scalar_tensor_tensor(
                    out=k[:],
                    in0=acc[:].rearrange("p (o n) -> p o n", o=1).to_broadcast([P, 2, CHUNK]),
                    scalar=bias[:, qk, g, e : e + 1],
                    in1=tabs[:, i, slots, :],
                    op0=ALU.add,
                    op1=ALU.mult,
                )
                return k

            if v_takes(n):
                vb = vpair(xb, 1, slice(1, 3), "vb")
                ga = vpair(xa, 0, slice(0, 2), "ga")
            else:
                a1 = work.tile([P, CHUNK], F32, name="a1")
                nc.scalar.activation(out=a1[:], in_=xa[:], func=ACT.Identity, bias=bias[:, qk, g, 0:1], scale=1.0)
                vb = vpair(xb, 1, slice(1, 3), "vb")
                ga = work.tile([P, 2, CHUNK], F32, name="ga")
                nc.gpsimd.tensor_tensor(
                    out=ga[:],
                    in0=a1[:].rearrange("p (o n) -> p o n", o=1).to_broadcast([P, 2, CHUNK]),
                    in1=tabs[:, i, 0:2, :],
                    op=ALU.mult,
                )
            live[("k", n)] = [(ga[:, 1, :], vb[:, 1, :]), (ga[:, 0, :], vb[:, 0, :])]

        def add_up(n, half):
            a, b = live[("k", n)][half]
            s = work.tile([P, CHUNK], F32, name="s%d" % half)
            nc.gpsimd.tensor_tensor(out=s[:], in0=a, in1=b, op=ALU.add)
            live[("k", n)][half] = (s[:],)

        def back(n):
            c, qk, g = steps[n]
            if g == 0:
                otiles[(c, qk)] = outp.tile([P, 4, D], F32, name="o")
            o = otiles[(c, qk)]
            ov = o[:].rearrange("p a (g hh half j) -> p a g hh half j", g=2, hh=2, half=2)
            if n == n_steps - 1:
                for ap in range(2):
                    tp = ps_tp.tile([P, CHUNK], F32, name="bt", tag="tp")
                    for al in range(2):
                        for half in range(2):
                            a = 2 * ap + al
                            blk = slice(a * P, (a + 1) * P)
                            terms = live[("k", n)][half]
                            lo = (2 * al + half) * P
                            for ti, t in enumerate(terms):
                                nc.tensor.matmul(
                                    out=tp[:, lo : lo + P],
                                    lhsT=t[:, blk],
                                    rhs=ident[:],
                                    is_transpose=True,
                                    start=(ti == 0),
                                    stop=(ti == len(terms) - 1),
                                )
                    dst = ov[:, 2 * ap : 2 * ap + 2, g]
                    for half in range(2):
                        srcv = tp[:].rearrange("p (a half hh j) -> p a half hh j", a=2, half=2, hh=2)[:, :, half]
                        if half == 0:
                            nc.scalar.copy(out=dst[:, :, :, half, :], in_=srcv)
                        else:
                            nc.vector.tensor_copy(out=dst[:, :, :, half, :], in_=srcv)
                    nc.sync.dma_start(
                        out=o_views[qk][c].rearrange("p (a g f) -> p a g f", a=4, g=2)[:, 2 * ap : 2 * ap + 2, g, :],
                        in_=o[:].rearrange("p a (g f) -> p a g f", g=2)[:, 2 * ap : 2 * ap + 2, g, :],
                    )
                return
            last = n >= n_steps - 2
            for half in range(2):
                tp = ps_tp.tile([P, CHUNK], F32, name="bt", tag="tp")
                for a in range(4):
                    blk = slice(a * P, (a + 1) * P)
                    terms = live[("k", n)][half]
                    for ti, t in enumerate(terms):
                        nc.tensor.matmul(
                            out=tp[:, blk],
                            lhsT=t[:, blk],
                            rhs=ident[:],
                            is_transpose=True,
                            start=(ti == 0),
                            stop=(ti == len(terms) - 1),
                        )
                dst = ov[:, :, g, :, half, :]
                srcv = tp[:].rearrange("p (a hh j) -> p a hh j", a=4, hh=2)
                if last and half == 1:
                    nc.vector.tensor_copy(out=dst, in_=srcv)
                else:
                    nc.scalar.copy(out=dst, in_=srcv)
            if n >= n_steps - 4:
                nc.sync.dma_start(
                    out=o_views[qk][c].rearrange("p (a g f) -> p a g f", a=4, g=2)[:, :, g, :],
                    in_=o[:].rearrange("p a (g f) -> p a g f", g=2)[:, :, g, :],
                )
            elif g == 1:
                nc.sync.dma_start(out=o_views[qk][c], in_=o[:].rearrange("p a f -> p (a f)"))

        x_cast(0, 0, 2, "v")
        x_cast(0, 2, 2, "s")
        x_turn(0, 0)
        x_mul(0, 0)
        w_turn(0, 0)
        x_turn(0, 1)
        w_turn(0, 1)
        w_quant(0, 0)
        x_mul(0, 1)
        tables_turn(0, 0)
        x_quant(0)
        nc.vector.tensor_copy(out=bias[:, 0], in_=braw_q[:])
        nc.vector.tensor_copy(out=bias[:, 1], in_=braw_k[:])
        tables_turn(0, 1)
        scales_spread()
        w_quant(0, 1)
        x_cast(1, 0, 4, "v")
        n_halves = 2 * N_CHUNKS
        for k in range((n_steps + LAG + 1) // 2):
            pair = (2 * k, 2 * k + 1)
            for n in pair:
                if n < n_steps:
                    front_mx(n)
            if k == 0:
                w_turn(1, 0)
                w_turn(1, 1)
                x_turn(1, 0)
            for n in pair:
                if n < n_steps:
                    front_mul(n)
                if n % 4 == 2 and n // 4 + 1 < N_CHUNKS:
                    x_quant(n // 4 + 1)
                if n == 0:
                    w_quant(1, 0)
                    w_quant(1, 1)
                    x_cast(2, 0, 4, "s")
                    x_mul(1, 0)
            if 11 <= k < 15:
                if v_takes(2 * k):
                    add_up(2 * k, 0)
                add_up(2 * k + 1, 1)
            for n in pair:
                if LAG <= n < n_steps + LAG:
                    back(n - LAG)
                if n % 2 == 0 and 8 <= k + 7 < n_halves:
                    x_cast((k + 7) // 2, 2 * ((k + 7) % 2), 2, "s")
            if k == 0:
                x_turn(1, 1)
                x_mul(1, 1)
                x_scale(2, 0)
                x_scale(2, 1)
                x_cast(3, 0, 2, "s")
                tables_turn(1, 0)
                tables_turn(1, 1)
            if 4 <= k + 3 < n_halves:
                x_turn_scaled((k + 3) // 2, (k + 3) % 2)
            if 6 <= k + 5 < n_halves:
                x_scale((k + 5) // 2, (k + 5) % 2)
            if k == 0:
                x_cast(3, 2, 2, "s")
